import numpy as np
import ml_dtypes


def mxq(x, axis, fmt="e4m3"):
    dtype, down = {"e4m3": (ml_dtypes.float8_e4m3fn, 7), "e5m2": (ml_dtypes.float8_e5m2, 14)}[fmt]
    v = np.moveaxis(np.asarray(x, np.float32).astype(ml_dtypes.bfloat16).astype(np.float64), axis, -1)
    blocks = v.reshape(v.shape[:-1] + (-1, 32))
    amax = np.abs(blocks).max(-1, keepdims=True)
    byte = np.maximum(np.where(amax > 0, np.frexp(amax)[1] - 1 + 127, 0) - down, 1)
    scale = np.exp2(byte - 127.0)
    codes = (blocks / scale).astype(np.float32).astype(dtype).astype(np.float64)
    return np.moveaxis((codes * scale).reshape(v.shape), -1, axis)


WIDE = False


def mx_kscale(k):
    if not WIDE:
        return np.ones(k)
    levels = np.array([10, -10, 5, -5, 0])
    if k % 512:
        return np.exp2(np.random.permutation(np.resize(levels, k // 32))).repeat(32)
    a = np.empty((k // 512, 16))
    for p in range(k // 512):
        a[p, :8] = np.random.permutation(np.resize(levels, 8))
        for g in range(8):
            far = levels[np.abs(levels - a[p, g]) >= 10]
            a[p, g + 8] = far[np.random.randint(len(far))]
    return np.exp2(a.ravel()).repeat(32)


BF16 = ml_dtypes.bfloat16


def bf(x):
    return np.asarray(x, np.float32).astype(BF16)


def f64(x):
    return np.asarray(x).astype(np.float64)


B, S, NI, NO = 16, 576, 256, 128


def setup_inputs():
    sn = mx_kscale(4 * NI)[::4]
    sc = NI ** -0.5

    def u():
        return bf(np.random.uniform(-sc, sc, (NO, NI)) / sn[None, :])

    return {"q_in": bf(np.random.standard_normal((B, S, 4 * NI)) * np.repeat(sn, 4)),
            "r_weight": u(), "i_weight": u(), "j_weight": u(), "k_weight": u()}


def reference(q_in, r_weight, i_weight, j_weight, k_weight):
    q = f64(q_in)
    V = np.stack([f64(r_weight), f64(i_weight), f64(j_weight), f64(k_weight)]).transpose(2, 0, 1).reshape(4 * NI, NO)
    Vq = mxq(V, 0, "e4m3")
    Wr, Wi, Wj, Wk = Vq.reshape(NI, 4, NO).transpose(1, 2, 0)
    W4 = np.stack([
        np.stack([Wr, -Wi, -Wj, -Wk]),
        np.stack([Wi, Wr, Wk, -Wj]),
        np.stack([Wj, -Wk, Wr, Wi]),
        np.stack([Wk, Wj, -Wi, Wr]),
    ])
    W = W4.transpose(3, 1, 2, 0).reshape(4 * NI, 4 * NO)
    return mxq(q, 2, "e4m3") @ W

@@ -1,0 +1,210 @@
+from contextlib import ExitStack
+
+import concourse.mybir as mybir
+from concourse.masks import make_identity
+
+BF16 = mybir.dt.bfloat16
+F32 = mybir.dt.float32
+U32 = mybir.dt.uint32
+U8 = mybir.dt.uint8
+FP8X4 = mybir.dt.float8_e4m3fn_x4
+
+P = 128
+TOKENS = 16 * 576
+K = 1024
+N_OUT = 512
+N_IN_Q = 256
+SLOTS = TOKENS // P
+FLOPS = 2 * TOKENS * K * N_OUT
+
+ROUNDS = [2, 2] + [4] * 17
+LOAD = 8
+X_BUFS = 6
+O_BUFS = 4
+MAXR = 4
+FIRST_LOADS = [1, 1, 2, 4]
+STORES = [4, 4] + [8] * 6 + [4, 4] + [2, 2, 2, 1, 1]
+MAXS = 8
+
+
+def tile_quaternionlinear_t_kernel(tc, q_in, r_weight, i_weight, j_weight, k_weight, out):
+    nc = tc.nc
+    assert sum(ROUNDS) == SLOTS
+    xin = q_in.flatten_outer_dims().rearrange("(p t) k -> p t k", t=SLOTS)
+    oview = out.flatten_outer_dims().rearrange("(p t) c -> p t c", t=SLOTS)
+
+    with ExitStack() as ctx:
+        const = ctx.enter_context(tc.tile_pool(name="const", bufs=1))
+        xpool = ctx.enter_context(tc.tile_pool(name="xpool", bufs=X_BUFS))
+        gpool = ctx.enter_context(tc.tile_pool(name="gpool", bufs=2))
+        cpool = ctx.enter_context(tc.tile_pool(name="cpool", bufs=3))
+        opool = ctx.enter_context(tc.tile_pool(name="opool", bufs=O_BUFS))
+        psum = ctx.enter_context(tc.psum_pool(name="psum", bufs=1))
+        ctx.enter_context(tc.manual_schedule())
+
+        ident = const.tile([P, P], F32, name="ident")
+        planes = const.tile([P, 11, N_IN_Q], BF16, name="planes")
+        wt = const.tile([P, 4, K], BF16, name="wt")
+        wgrp = const.tile([P, 2, 4 * N_OUT], BF16, name="wgrp", align_bytes=64)
+        wcodes = const.tile([P, 2, N_OUT], U32, name="wcodes", align_bytes=64)
+        wscl = const.tile([P, 2, N_OUT], U8, name="wscl", align_bytes=64)
+
+        for pos, w in ((0, i_weight), (3, j_weight), (1, k_weight), (4, r_weight)):
+            nc.sync.dma_start(out=planes[:, pos, :], in_=w)
+
+        n_chunks = SLOTS // LOAD
+        xt = {}
+
+        def load(c):
+            x_sb = xpool.tile([P, LOAD, K], BF16, name="x_sb", tag="x")
+            xt[c] = x_sb
+            if c == 0:
+                lo = 0
+                for n in FIRST_LOADS:
+                    nc.sync.dma_start(out=x_sb[:, lo:lo + n, :], in_=xin[:, lo:lo + n, :])
+                    lo += n
+            else:
+                nc.sync.dma_start(out=x_sb[:], in_=xin[:, c * LOAD:(c + 1) * LOAD, :])
+
+        for c in range(min(X_BUFS, n_chunks)):
+            load(c)
+
+        make_identity(nc, ident[:])
+
+        nc.vector.tensor_scalar_mul(out=planes[:, 2:6:3, :], in0=planes[:, 0:4:3, :], scalar1=-1.0)
+        nc.vector.tensor_scalar_mul(out=planes[:, 6:8, :], in0=planes[:, 0:2, :], scalar1=-1.0)
+        nc.scalar.copy(out=planes[:, 8, :], in_=planes[:, 0, :])
+
+        def near(b):
+            return planes[:, b:b + 4, :].rearrange("p (e a) n -> p n a e", e=2)
+
+        def far(b):
+            v = planes[:, b:b + 8, :].rearrange("p (e x) n -> p e x n", e=2)
+            return v[:, :, 0:2, :].rearrange("p e a n -> p n a e")
+
+        def wt_view(d):
+            return wt[:, d, :].rearrange("p (n a e) -> p n a e", a=2, e=2)
+
+        nc.vector.tensor_copy(out=wt_view(1), in_=far(0))
+        nc.scalar.copy(out=wt_view(2), in_=far(3))
+        nc.vector.tensor_copy(out=wt_view(0), in_=near(4))
+        nc.vector.tensor_copy(out=wt_view(3), in_=near(1))
+
+        wgw = wgrp[:].bitcast(F32).rearrange("p g (m d x) -> p g m d x", d=2, x=4)
+
+        def weight_half(d1):
+            banks = []
+            for g in range(2):
+                wb = psum.tile([P, 4, P], F32, name="wb", tag="op%d" % (2 * d1 + g))
+                banks.append(wb)
+                for d0 in range(2):
+                    for u in range(2):
+                        nc.tensor.transpose(
+                            out=wb[:, 2 * d0 + u, :],
+                            in_=wt[:, 2 * d1 + d0, :].bitcast(F32)[:, 256 * g + u:256 * (g + 1):2],
+                            identity=ident[:],
+                        )
+            nc.vector.tensor_copy(out=wgw[:, 0, :, d1, :], in_=banks[0][:].rearrange("p x m -> p m x"))
+            nc.scalar.copy(out=wgw[:, 1, :, d1, :], in_=banks[1][:].rearrange("p x m -> p m x"))
+
+        starts = [sum(ROUNDS[:r]) for r in range(len(ROUNDS))]
+        n_rounds = len(ROUNDS)
+        tps = {}
+        grps = {}
+        cods = {}
+        next_load = [min(X_BUFS, n_chunks)]
+
+        def transposes(r):
+            for j in range(ROUNDS[r]):
+                t = starts[r] + j
+                c, l = divmod(t, LOAD)
+                tp = psum.tile([P, 4, P], F32, name="tp", tag="tp%d" % j)
+                tps[(r, j)] = tp
+                xw = xt[c][:, l, :].bitcast(F32)
+                for s in range(4):
+                    nc.tensor.transpose(out=tp[:, s, :], in_=xw[:, 256 * (s // 2) + s % 2:256 * (s // 2 + 1):2], identity=ident[:])
+                if l == LOAD - 1 and next_load[0] < n_chunks:
+                    load(next_load[0])
+                    next_load[0] += 1
+
+        def copies(r):
+            n = ROUNDS[r]
+            grp = gpool.tile([P, MAXR * K], BF16, name="grp", tag="grp", align_bytes=64)
+            grps[r] = grp
+            gw = grp[:].bitcast(F32).rearrange("p (j g k u) -> p j g k u", j=MAXR, g=2, u=2)
+            for j in range(n):
+                src = tps[(r, j)][:].rearrange("p (g u) k -> p g k u", g=2)
+                if r > 0 and j < (n + 1) // 2:
+                    nc.vector.tensor_copy(out=gw[:, j, :, :, :], in_=src)
+                else:
+                    nc.scalar.copy(out=gw[:, j, :, :, :], in_=src)
+
+        def quantise(r):
+            n = ROUNDS[r]
+            codes = cpool.tile([P, MAXR * 256], U32, name="codes", tag="codes", align_bytes=64)
+            scl = cpool.tile([P, MAXR * 256], U8, name="scl", tag="scl", align_bytes=64)
+            cods[r] = (codes, scl)
+            nc.vector.quantize_mx(
+                out=codes[:, 0:n * 256].bitcast(FP8X4),
+                scales=scl[:, 0:n * 256],
+                in_=grps[r][:, 0:n * K],
+            )
+
+        def multiply(r):
+            n = ROUNDS[r]
+            codes, scl = cods[r]
+            for j in range(n):
+                acc = psum.tile([P, N_OUT], F32, name="acc", tag="op%d" % j)
+                for g in range(2):
+                    o = (2 * j + g) * P
+                    nc.tensor.matmul_mx(
+                        out=acc[:],
+                        lhsT=codes[:, o:o + P].bitcast(FP8X4),
+                        lhsT_scale=scl[:, o:o + P],
+                        rhs=wcodes[:, g, :].bitcast(FP8X4),
+                        rhs_scale=wscl[:, g, :],
+                        start=(g == 0),
+                        stop=(g == 1),
+                    )
+                tps[("o", r, j)] = acc
+
+        group_of = {}
+        lo = 0
+        for n in STORES:
+            for t in range(lo, lo + n):
+                group_of[t] = (lo, n)
+            lo += n
+        assert lo == SLOTS
+        cur = {}
+
+        def drain(r):
+            for j in range(ROUNDS[r]):
+                t = starts[r] + j
+                g0, gn = group_of[t]
+                if t % MAXS == 0:
+                    cur["osb"] = opool.tile([P, MAXS, N_OUT], F32, name="osb", tag="osb")
+                osb = cur["osb"]
+                b = t % MAXS
+                acc = tps[("o", r, j)]
+                if j == 2:
+                    nc.vector.tensor_copy(out=osb[:, b, :], in_=acc[:])
+                else:
+                    nc.scalar.copy(out=osb[:, b, :], in_=acc[:])
+                if t == g0 + gn - 1:
+                    nc.sync.dma_start(out=oview[:, g0:g0 + gn, :], in_=osb[:, b + 1 - gn:b + 1, :])
+
+        transposes(0)
+        copies(0)
+        weight_half(0)
+        quantise(0)
+        weight_half(1)
+        for g in range(2):
+            nc.vector.quantize_mx(out=wcodes[:, g, :].bitcast(FP8X4), scales=wscl[:, g, :], in_=wgrp[:, g, :])
+        for r in range(n_rounds):
+            if r + 1 < n_rounds:
+                transposes(r + 1)
+                copies(r + 1)
+            multiply(r)
+            if r + 1 < n_rounds:
+                quantise(r + 1)
+            drain(r)

@@ -22,6 +22,7 @@ LOAD = 8
 X_BUFS = 6
 O_BUFS = 4
 MAXR = 4
+FIRST_PERMUTED = 2
 FIRST_LOADS = [1, 1, 2, 4]
 STORES = [4, 4] + [8] * 6 + [4, 4] + [2, 2, 2, 1, 1]
 MAXS = 8
@@ -36,6 +37,7 @@ def tile_quaternionlinear_t_kernel(tc, q_in, r_weight, i_weight, j_weight, k_wei
     with ExitStack() as ctx:
         const = ctx.enter_context(tc.tile_pool(name="const", bufs=1))
         xpool = ctx.enter_context(tc.tile_pool(name="xpool", bufs=X_BUFS))
+        ppool = ctx.enter_context(tc.tile_pool(name="ppool", bufs=2))
         gpool = ctx.enter_context(tc.tile_pool(name="gpool", bufs=2))
         cpool = ctx.enter_context(tc.tile_pool(name="cpool", bufs=3))
         opool = ctx.enter_context(tc.tile_pool(name="opool", bufs=O_BUFS))
@@ -114,18 +116,36 @@ def tile_quaternionlinear_t_kernel(tc, q_in, r_weight, i_weight, j_weight, k_wei
         cods = {}
         next_load = [min(X_BUFS, n_chunks)]
 
+        perms = {}
+
+        def permute(r):
+            if r < FIRST_PERMUTED:
+                return
+            n = ROUNDS[r]
+            c, l = divmod(starts[r], LOAD)
+            xp = ppool.tile([P, MAXR, 2, 256], F32, name="xp", tag="xp")
+            perms[r] = xp
+            nc.vector.tensor_copy(
+                out=xp[:, 0:n, :, :],
+                in_=xt[c][:, l:l + n, :].bitcast(F32).rearrange("p j (w u) -> p j u w", u=2),
+            )
+            if l + n == LOAD and next_load[0] < n_chunks:
+                load(next_load[0])
+                next_load[0] += 1
+
         def transposes(r):
             for j in range(ROUNDS[r]):
                 t = starts[r] + j
                 c, l = divmod(t, LOAD)
                 tp = psum.tile([P, 4, P], F32, name="tp", tag="tp%d" % j)
                 tps[(r, j)] = tp
-                xw = xt[c][:, l, :].bitcast(F32)
-                for s in range(4):
-                    nc.tensor.transpose(out=tp[:, s, :], in_=xw[:, 256 * (s // 2) + s % 2:256 * (s // 2 + 1):2], identity=ident[:])
-                if l == LOAD - 1 and next_load[0] < n_chunks:
-                    load(next_load[0])
-                    next_load[0] += 1
+                for g in range(2):
+                    for u in range(2):
+                        if r < FIRST_PERMUTED:
+                            words = xt[c][:, l, :].bitcast(F32)[:, 256 * g + u:256 * (g + 1):2]
+                        else:
+                            words = perms[r][:, j, u, g * P:(g + 1) * P]
+                        nc.tensor.transpose(out=tp[:, 2 * g + u, :], in_=words, identity=ident[:])
 
         def copies(r):
             n = ROUNDS[r]
@@ -134,7 +154,7 @@ def tile_quaternionlinear_t_kernel(tc, q_in, r_weight, i_weight, j_weight, k_wei
             gw = grp[:].bitcast(F32).rearrange("p (j g k u) -> p j g k u", j=MAXR, g=2, u=2)
             for j in range(n):
                 src = tps[(r, j)][:].rearrange("p (g u) k -> p g k u", g=2)
-                if r > 0 and j < (n + 1) // 2:
+                if r > 0 and j < (1 if n == 4 else (n + 1) // 2):
                     nc.vector.tensor_copy(out=gw[:, j, :, :, :], in_=src)
                 else:
                     nc.scalar.copy(out=gw[:, j, :, :, :], in_=src)
@@ -204,6 +224,8 @@ def tile_quaternionlinear_t_kernel(tc, q_in, r_weight, i_weight, j_weight, k_wei
             if r + 1 < n_rounds:
                 transposes(r + 1)
                 copies(r + 1)
+            if r + 2 < n_rounds:
+                permute(r + 2)
             multiply(r)
             if r + 1 < n_rounds:
                 quantise(r + 1)

@@ -78,14 +78,14 @@ def tile_quaternionlinear_t_kernel(tc, q_in, r_weight, i_weight, j_weight, k_wei
         nc.scalar.copy(out=planes[:, 8, :], in_=planes[:, 0, :])
 
         def near(b):
-            return planes[:, b:b + 4, :].rearrange("p (e a) n -> p n a e", e=2)
+            return planes[:, b:b + 4, :].rearrange("p (e a) n -> p a n e", e=2)
 
         def far(b):
             v = planes[:, b:b + 8, :].rearrange("p (e x) n -> p e x n", e=2)
-            return v[:, :, 0:2, :].rearrange("p e a n -> p n a e")
+            return v[:, :, 0:2, :].rearrange("p e a n -> p a n e")
 
         def wt_view(d):
-            return wt[:, d, :].rearrange("p (n a e) -> p n a e", a=2, e=2)
+            return wt[:, d, :].rearrange("p (a n e) -> p a n e", a=2, e=2)
 
         nc.vector.tensor_copy(out=wt_view(1), in_=far(0))
         nc.scalar.copy(out=wt_view(2), in_=far(3))
@@ -103,7 +103,7 @@ def tile_quaternionlinear_t_kernel(tc, q_in, r_weight, i_weight, j_weight, k_wei
                     for u in range(2):
                         nc.tensor.transpose(
                             out=wb[:, 2 * d0 + u, :],
-                            in_=wt[:, 2 * d1 + d0, :].bitcast(F32)[:, 256 * g + u:256 * (g + 1):2],
+                            in_=wt[:, 2 * d1 + d0, :].bitcast(F32)[:, 256 * u + g * P:256 * u + (g + 1) * P],
                             identity=ident[:],
                         )
             nc.vector.tensor_copy(out=wgw[:, 0, :, d1, :], in_=banks[0][:].rearrange("p x m -> p m x"))
@@ -133,8 +133,8 @@ def tile_quaternionlinear_t_kernel(tc, q_in, r_weight, i_weight, j_weight, k_wei
                 load(next_load[0])
                 next_load[0] += 1
 
-        def transposes(r):
-            for j in range(ROUNDS[r]):
+        def transposes(r, js=None):
+            for j in js or range(ROUNDS[r]):
                 t = starts[r] + j
                 c, l = divmod(t, LOAD)
                 tp = psum.tile([P, 4, P], F32, name="tp", tag="tp%d" % j)
@@ -147,12 +147,12 @@ def tile_quaternionlinear_t_kernel(tc, q_in, r_weight, i_weight, j_weight, k_wei
                             words = perms[r][:, j, u, g * P:(g + 1) * P]
                         nc.tensor.transpose(out=tp[:, 2 * g + u, :], in_=words, identity=ident[:])
 
-        def copies(r):
+        def copies(r, js=None):
             n = ROUNDS[r]
-            grp = gpool.tile([P, MAXR * K], BF16, name="grp", tag="grp", align_bytes=64)
-            grps[r] = grp
-            gw = grp[:].bitcast(F32).rearrange("p (j g k u) -> p j g k u", j=MAXR, g=2, u=2)
-            for j in range(n):
+            if r not in grps:
+                grps[r] = gpool.tile([P, MAXR * K], BF16, name="grp", tag="grp", align_bytes=64)
+            gw = grps[r][:].bitcast(F32).rearrange("p (j g k u) -> p j g k u", j=MAXR, g=2, u=2)
+            for j in js or range(n):
                 src = tps[(r, j)][:].rearrange("p (g u) k -> p g k u", g=2)
                 if r > 0 and j < (1 if n == 4 else (n + 1) // 2):
                     nc.vector.tensor_copy(out=gw[:, j, :, :, :], in_=src)
@@ -213,13 +213,18 @@ def tile_quaternionlinear_t_kernel(tc, q_in, r_weight, i_weight, j_weight, k_wei
                 if t == g0 + gn - 1:
                     nc.sync.dma_start(out=oview[:, g0:g0 + gn, :], in_=osb[:, b + 1 - gn:b + 1, :])
 
-        transposes(0)
-        copies(0)
-        weight_half(0)
-        quantise(0)
-        weight_half(1)
-        for g in range(2):
+        def quantise_weights(g):
             nc.vector.quantize_mx(out=wcodes[:, g, :].bitcast(FP8X4), scales=wscl[:, g, :], in_=wgrp[:, g, :])
+
+        transposes(0, [0])
+        copies(0, [0])
+        weight_half(0)
+        transposes(0, [1])
+        copies(0, [1])
+        weight_half(1)
+        quantise_weights(0)
+        quantise(0)
+        quantise_weights(1)
         for r in range(n_rounds):
             if r + 1 < n_rounds:
                 transposes(r + 1)

@@ -126,8 +126,8 @@ def tile_quaternionlinear_t_kernel(tc, q_in, r_weight, i_weight, j_weight, k_wei
             xp = ppool.tile([P, MAXR, 2, 256], F32, name="xp", tag="xp")
             perms[r] = xp
             nc.vector.tensor_copy(
-                out=xp[:, 0:n, :, :],
-                in_=xt[c][:, l:l + n, :].bitcast(F32).rearrange("p j (w u) -> p j u w", u=2),
+                out=xp[:, 0:n, :, :].rearrange("p j u (b i) -> p j b u i", i=4),
+                in_=xt[c][:, l:l + n, :].bitcast(F32).rearrange("p j (b i u) -> p j b u i", i=4, u=2),
             )
             if l + n == LOAD and next_load[0] < n_chunks:
                 load(next_load[0])

@@ -18,60 +18,64 @@ SLOTS = TOKENS // P
 FLOPS = 2 * TOKENS * K * N_OUT
 
 ROUNDS = [2, 2] + [4] * 17
-LOAD = 8
-X_BUFS = 6
-O_BUFS = 4
 MAXR = 4
 FIRST_PERMUTED = 2
-FIRST_LOADS = [1, 1, 2, 4]
-STORES = [4, 4] + [8] * 6 + [4, 4] + [2, 2, 2, 1, 1]
-MAXS = 8
+X_SLOTS = 48
+O_SLOTS = 32
+LOADS = [1, 1, 2, 4, 4, 8, 12, 16] + [16, 8]
+STORES = [16, 16, 16, 8, 4, 4, 4, 2, 1, 1]
+WARM_FIRST = 4
+WARM_BETWEEN = 1
+WARM_LAST = 2
+ALIGN = 256
 
 
 def tile_quaternionlinear_t_kernel(tc, q_in, r_weight, i_weight, j_weight, k_weight, out):
     nc = tc.nc
     assert sum(ROUNDS) == SLOTS
+    assert sum(LOADS) == SLOTS
+    assert sum(STORES) == SLOTS
     xin = q_in.flatten_outer_dims().rearrange("(p t) k -> p t k", t=SLOTS)
     oview = out.flatten_outer_dims().rearrange("(p t) c -> p t c", t=SLOTS)
 
     with ExitStack() as ctx:
         const = ctx.enter_context(tc.tile_pool(name="const", bufs=1))
-        xpool = ctx.enter_context(tc.tile_pool(name="xpool", bufs=X_BUFS))
         ppool = ctx.enter_context(tc.tile_pool(name="ppool", bufs=2))
-        gpool = ctx.enter_context(tc.tile_pool(name="gpool", bufs=2))
+        gpool = ctx.enter_context(tc.tile_pool(name="gpool", bufs=3))
         cpool = ctx.enter_context(tc.tile_pool(name="cpool", bufs=3))
-        opool = ctx.enter_context(tc.tile_pool(name="opool", bufs=O_BUFS))
         psum = ctx.enter_context(tc.psum_pool(name="psum", bufs=1))
         ctx.enter_context(tc.manual_schedule())
 
-        ident = const.tile([P, P], F32, name="ident")
-        planes = const.tile([P, 11, N_IN_Q], BF16, name="planes")
-        wt = const.tile([P, 4, K], BF16, name="wt")
-        wgrp = const.tile([P, 2, 4 * N_OUT], BF16, name="wgrp", align_bytes=64)
-        wcodes = const.tile([P, 2, N_OUT], U32, name="wcodes", align_bytes=64)
-        wscl = const.tile([P, 2, N_OUT], U8, name="wscl", align_bytes=64)
+        ident = const.tile([P, P], F32, name="ident", align_bytes=ALIGN)
+        zeros = const.tile([P, N_OUT], BF16, name="zeros", align_bytes=ALIGN)
+        planes = const.tile([P, 11, N_IN_Q], BF16, name="planes", align_bytes=ALIGN)
+        wcodes = const.tile([P, 2, N_OUT], U32, name="wcodes", align_bytes=ALIGN)
+        wscl = const.tile([P, 2, N_OUT], U8, name="wscl", align_bytes=ALIGN)
+        xring = const.tile([P, X_SLOTS, K], BF16, name="xring", align_bytes=ALIGN)
+        oring = const.tile([P, O_SLOTS, N_OUT], F32, name="oring", align_bytes=ALIGN)
+        wt = gpool.tile([P, 4, K], BF16, name="wt", tag="grp", align_bytes=ALIGN)
+        wgrp = gpool.tile([P, 2, 4 * N_OUT], BF16, name="wgrp", tag="grp", align_bytes=ALIGN)
 
         for pos, w in ((0, i_weight), (3, j_weight), (1, k_weight), (4, r_weight)):
             nc.sync.dma_start(out=planes[:, pos, :], in_=w)
 
-        n_chunks = SLOTS // LOAD
-        xt = {}
+        pending = [(sum(LOADS[:i]), n) for i, n in enumerate(LOADS)]
 
-        def load(c):
-            x_sb = xpool.tile([P, LOAD, K], BF16, name="x_sb", tag="x")
-            xt[c] = x_sb
-            if c == 0:
-                lo = 0
-                for n in FIRST_LOADS:
-                    nc.sync.dma_start(out=x_sb[:, lo:lo + n, :], in_=xin[:, lo:lo + n, :])
-                    lo += n
-            else:
-                nc.sync.dma_start(out=x_sb[:], in_=xin[:, c * LOAD:(c + 1) * LOAD, :])
+        def load():
+            t, n = pending.pop(0)
+            s = t % X_SLOTS
+            nc.sync.dma_start(out=xring[:, s:s + n, :], in_=xin[:, t:t + n, :])
 
-        for c in range(min(X_BUFS, n_chunks)):
-            load(c)
+        while pending[0][0] < X_SLOTS:
+            load()
 
+        nc.gpsimd.memset(zeros[:], 0.0)
         make_identity(nc, ident[:])
+
+        def warm(n):
+            wm = psum.tile([P, N_OUT], F32, name="wm", tag="tp3")
+            for i in range(n):
+                nc.tensor.matmul(wm[:], lhsT=zeros[:, 0:P], rhs=zeros[:], start=True, stop=True)
 
         nc.vector.tensor_scalar_mul(out=planes[:, 2:6:3, :], in0=planes[:, 0:4:3, :], scalar1=-1.0)
         nc.vector.tensor_scalar_mul(out=planes[:, 6:8, :], in0=planes[:, 0:2, :], scalar1=-1.0)
@@ -106,7 +110,10 @@ def tile_quaternionlinear_t_kernel(tc, q_in, r_weight, i_weight, j_weight, k_wei
                             in_=wt[:, 2 * d1 + d0, :].bitcast(F32)[:, 256 * u + g * P:256 * u + (g + 1) * P],
                             identity=ident[:],
                         )
-            nc.vector.tensor_copy(out=wgw[:, 0, :, d1, :], in_=banks[0][:].rearrange("p x m -> p m x"))
+            if d1 == 0:
+                nc.vector.tensor_copy(out=wgw[:, 0, :, d1, :], in_=banks[0][:].rearrange("p x m -> p m x"))
+            else:
+                nc.scalar.copy(out=wgw[:, 0, :, d1, :], in_=banks[0][:].rearrange("p x m -> p m x"))
             nc.scalar.copy(out=wgw[:, 1, :, d1, :], in_=banks[1][:].rearrange("p x m -> p m x"))
 
         starts = [sum(ROUNDS[:r]) for r in range(len(ROUNDS))]
@@ -114,7 +121,6 @@ def tile_quaternionlinear_t_kernel(tc, q_in, r_weight, i_weight, j_weight, k_wei
         tps = {}
         grps = {}
         cods = {}
-        next_load = [min(X_BUFS, n_chunks)]
 
         perms = {}
 
@@ -122,37 +128,33 @@ def tile_quaternionlinear_t_kernel(tc, q_in, r_weight, i_weight, j_weight, k_wei
             if r < FIRST_PERMUTED:
                 return
             n = ROUNDS[r]
-            c, l = divmod(starts[r], LOAD)
+            s = starts[r] % X_SLOTS
             xp = ppool.tile([P, MAXR, 2, 256], F32, name="xp", tag="xp")
             perms[r] = xp
             nc.vector.tensor_copy(
                 out=xp[:, 0:n, :, :].rearrange("p j u (b i) -> p j b u i", i=4),
-                in_=xt[c][:, l:l + n, :].bitcast(F32).rearrange("p j (b i u) -> p j b u i", i=4, u=2),
+                in_=xring[:, s:s + n, :].bitcast(F32).rearrange("p j (b i u) -> p j b u i", i=4, u=2),
             )
-            if l + n == LOAD and next_load[0] < n_chunks:
-                load(next_load[0])
-                next_load[0] += 1
 
-        def transposes(r, js=None):
-            for j in js or range(ROUNDS[r]):
-                t = starts[r] + j
-                c, l = divmod(t, LOAD)
+        def transposes(r):
+            for j in range(ROUNDS[r]):
+                s = (starts[r] + j) % X_SLOTS
                 tp = psum.tile([P, 4, P], F32, name="tp", tag="tp%d" % j)
                 tps[(r, j)] = tp
                 for g in range(2):
                     for u in range(2):
                         if r < FIRST_PERMUTED:
-                            words = xt[c][:, l, :].bitcast(F32)[:, 256 * g + u:256 * (g + 1):2]
+                            words = xring[:, s, :].bitcast(F32)[:, 256 * g + u:256 * (g + 1):2]
                         else:
                             words = perms[r][:, j, u, g * P:(g + 1) * P]
                         nc.tensor.transpose(out=tp[:, 2 * g + u, :], in_=words, identity=ident[:])
 
-        def copies(r, js=None):
+        def copies(r):
             n = ROUNDS[r]
             if r not in grps:
-                grps[r] = gpool.tile([P, MAXR * K], BF16, name="grp", tag="grp", align_bytes=64)
+                grps[r] = gpool.tile([P, MAXR * K], BF16, name="grp", tag="grp", align_bytes=ALIGN)
             gw = grps[r][:].bitcast(F32).rearrange("p (j g k u) -> p j g k u", j=MAXR, g=2, u=2)
-            for j in js or range(n):
+            for j in range(n):
                 src = tps[(r, j)][:].rearrange("p (g u) k -> p g k u", g=2)
                 if r > 0 and j < (1 if n == 4 else (n + 1) // 2):
                     nc.vector.tensor_copy(out=gw[:, j, :, :, :], in_=src)
@@ -161,8 +163,8 @@ def tile_quaternionlinear_t_kernel(tc, q_in, r_weight, i_weight, j_weight, k_wei
 
         def quantise(r):
             n = ROUNDS[r]
-            codes = cpool.tile([P, MAXR * 256], U32, name="codes", tag="codes", align_bytes=64)
-            scl = cpool.tile([P, MAXR * 256], U8, name="scl", tag="scl", align_bytes=64)
+            codes = cpool.tile([P, MAXR * 256], U32, name="codes", tag="codes", align_bytes=ALIGN)
+            scl = cpool.tile([P, MAXR * 256], U8, name="scl", tag="scl", align_bytes=ALIGN)
             cods[r] = (codes, scl)
             nc.vector.quantize_mx(
                 out=codes[:, 0:n * 256].bitcast(FP8X4),
@@ -188,47 +190,42 @@ def tile_quaternionlinear_t_kernel(tc, q_in, r_weight, i_weight, j_weight, k_wei
                     )
                 tps[("o", r, j)] = acc
 
-        group_of = {}
+        store_from = {}
         lo = 0
         for n in STORES:
-            for t in range(lo, lo + n):
-                group_of[t] = (lo, n)
+            store_from[lo + n - 1] = lo
             lo += n
-        assert lo == SLOTS
-        cur = {}
 
         def drain(r):
             for j in range(ROUNDS[r]):
                 t = starts[r] + j
-                g0, gn = group_of[t]
-                if t % MAXS == 0:
-                    cur["osb"] = opool.tile([P, MAXS, N_OUT], F32, name="osb", tag="osb")
-                osb = cur["osb"]
-                b = t % MAXS
+                s = t % O_SLOTS
                 acc = tps[("o", r, j)]
                 if j == 2:
-                    nc.vector.tensor_copy(out=osb[:, b, :], in_=acc[:])
+                    nc.vector.tensor_copy(out=oring[:, s, :], in_=acc[:])
                 else:
-                    nc.scalar.copy(out=osb[:, b, :], in_=acc[:])
-                if t == g0 + gn - 1:
-                    nc.sync.dma_start(out=oview[:, g0:g0 + gn, :], in_=osb[:, b + 1 - gn:b + 1, :])
+                    nc.scalar.copy(out=oring[:, s, :], in_=acc[:])
+                if t in store_from:
+                    lo = store_from[t]
+                    nc.sync.dma_start(out=oview[:, lo:t + 1, :], in_=oring[:, s - (t - lo):s + 1, :])
+                    if pending and pending[0][0] - O_SLOTS <= t + 1:
+                        load()
 
-        def quantise_weights(g):
-            nc.vector.quantize_mx(out=wcodes[:, g, :].bitcast(FP8X4), scales=wscl[:, g, :], in_=wgrp[:, g, :])
-
-        transposes(0, [0])
-        copies(0, [0])
+        warm(WARM_FIRST)
+        transposes(0)
+        copies(0)
         weight_half(0)
-        transposes(0, [1])
-        copies(0, [1])
-        weight_half(1)
-        quantise_weights(0)
         quantise(0)
-        quantise_weights(1)
+        warm(WARM_BETWEEN)
+        weight_half(1)
+        for g in range(2):
+            nc.vector.quantize_mx(out=wcodes[:, g, :].bitcast(FP8X4), scales=wscl[:, g, :], in_=wgrp[:, g, :])
         for r in range(n_rounds):
             if r + 1 < n_rounds:
                 transposes(r + 1)
                 copies(r + 1)
+            if r == 0:
+                warm(WARM_LAST)
             if r + 2 < n_rounds:
                 permute(r + 2)
             multiply(r)

from contextlib import ExitStack

import concourse.mybir as mybir
from concourse.masks import make_identity

BF16 = mybir.dt.bfloat16
F32 = mybir.dt.float32
U32 = mybir.dt.uint32
U8 = mybir.dt.uint8
FP8X4 = mybir.dt.float8_e4m3fn_x4

P = 128
TOKENS = 16 * 576
K = 1024
N_OUT = 512
N_IN_Q = 256
SLOTS = TOKENS // P
FLOPS = 2 * TOKENS * K * N_OUT

ROUNDS = [2, 2] + [4] * 17
MAXR = 4
FIRST_PERMUTED = 2
X_SLOTS = 48
O_SLOTS = 32
LOADS = [1, 1, 2, 4, 4, 8, 12, 16] + [16, 8]
STORES = [16, 16, 16, 8, 4, 4, 4, 2, 1, 1]
WARM_FIRST = 4
WARM_BETWEEN = 1
WARM_LAST = 2
ALIGN = 256


def tile_quaternionlinear_t_kernel(tc, q_in, r_weight, i_weight, j_weight, k_weight, out):
    nc = tc.nc
    assert sum(ROUNDS) == SLOTS
    assert sum(LOADS) == SLOTS
    assert sum(STORES) == SLOTS
    xin = q_in.flatten_outer_dims().rearrange("(p t) k -> p t k", t=SLOTS)
    oview = out.flatten_outer_dims().rearrange("(p t) c -> p t c", t=SLOTS)

    with ExitStack() as ctx:
        const = ctx.enter_context(tc.tile_pool(name="const", bufs=1))
        ppool = ctx.enter_context(tc.tile_pool(name="ppool", bufs=2))
        gpool = ctx.enter_context(tc.tile_pool(name="gpool", bufs=3))
        cpool = ctx.enter_context(tc.tile_pool(name="cpool", bufs=3))
        psum = ctx.enter_context(tc.psum_pool(name="psum", bufs=1))
        ctx.enter_context(tc.manual_schedule())

        ident = const.tile([P, P], F32, name="ident", align_bytes=ALIGN)
        zeros = const.tile([P, N_OUT], BF16, name="zeros", align_bytes=ALIGN)
        planes = const.tile([P, 11, N_IN_Q], BF16, name="planes", align_bytes=ALIGN)
        wcodes = const.tile([P, 2, N_OUT], U32, name="wcodes", align_bytes=ALIGN)
        wscl = const.tile([P, 2, N_OUT], U8, name="wscl", align_bytes=ALIGN)
        xring = const.tile([P, X_SLOTS, K], BF16, name="xring", align_bytes=ALIGN)
        oring = const.tile([P, O_SLOTS, N_OUT], F32, name="oring", align_bytes=ALIGN)
        wt = gpool.tile([P, 4, K], BF16, name="wt", tag="grp", align_bytes=ALIGN)
        wgrp = gpool.tile([P, 2, 4 * N_OUT], BF16, name="wgrp", tag="grp", align_bytes=ALIGN)

        for pos, w in ((0, i_weight), (3, j_weight), (1, k_weight), (4, r_weight)):
            nc.sync.dma_start(out=planes[:, pos, :], in_=w)

        pending = [(sum(LOADS[:i]), n) for i, n in enumerate(LOADS)]

        def load():
            t, n = pending.pop(0)
            s = t % X_SLOTS
            nc.sync.dma_start(out=xring[:, s:s + n, :], in_=xin[:, t:t + n, :])

        while pending[0][0] < X_SLOTS:
            load()

        nc.gpsimd.memset(zeros[:], 0.0)
        make_identity(nc, ident[:])

        def warm(n):
            wm = psum.tile([P, N_OUT], F32, name="wm", tag="tp3")
            for i in range(n):
                nc.tensor.matmul(wm[:], lhsT=zeros[:, 0:P], rhs=zeros[:], start=True, stop=True)

        nc.vector.tensor_scalar_mul(out=planes[:, 2:6:3, :], in0=planes[:, 0:4:3, :], scalar1=-1.0)
        nc.vector.tensor_scalar_mul(out=planes[:, 6:8, :], in0=planes[:, 0:2, :], scalar1=-1.0)
        nc.scalar.copy(out=planes[:, 8, :], in_=planes[:, 0, :])

        def near(b):
            return planes[:, b:b + 4, :].rearrange("p (e a) n -> p a n e", e=2)

        def far(b):
            v = planes[:, b:b + 8, :].rearrange("p (e x) n -> p e x n", e=2)
            return v[:, :, 0:2, :].rearrange("p e a n -> p a n e")

        def wt_view(d):
            return wt[:, d, :].rearrange("p (a n e) -> p a n e", a=2, e=2)

        nc.vector.tensor_copy(out=wt_view(1), in_=far(0))
        nc.scalar.copy(out=wt_view(2), in_=far(3))
        nc.vector.tensor_copy(out=wt_view(0), in_=near(4))
        nc.vector.tensor_copy(out=wt_view(3), in_=near(1))

        wgw = wgrp[:].bitcast(F32).rearrange("p g (m d x) -> p g m d x", d=2, x=4)

        def weight_half(d1):
            banks = []
            for g in range(2):
                wb = psum.tile([P, 4, P], F32, name="wb", tag="op%d" % (2 * d1 + g))
                banks.append(wb)
                for d0 in range(2):
                    for u in range(2):
                        nc.tensor.transpose(
                            out=wb[:, 2 * d0 + u, :],
                            in_=wt[:, 2 * d1 + d0, :].bitcast(F32)[:, 256 * u + g * P:256 * u + (g + 1) * P],
                            identity=ident[:],
                        )
            if d1 == 0:
                nc.vector.tensor_copy(out=wgw[:, 0, :, d1, :], in_=banks[0][:].rearrange("p x m -> p m x"))
            else:
                nc.scalar.copy(out=wgw[:, 0, :, d1, :], in_=banks[0][:].rearrange("p x m -> p m x"))
            nc.scalar.copy(out=wgw[:, 1, :, d1, :], in_=banks[1][:].rearrange("p x m -> p m x"))

        starts = [sum(ROUNDS[:r]) for r in range(len(ROUNDS))]
        n_rounds = len(ROUNDS)
        tps = {}
        grps = {}
        cods = {}

        perms = {}

        def permute(r):
            if r < FIRST_PERMUTED:
                return
            n = ROUNDS[r]
            s = starts[r] % X_SLOTS
            xp = ppool.tile([P, MAXR, 2, 256], F32, name="xp", tag="xp")
            perms[r] = xp
            nc.vector.tensor_copy(
                out=xp[:, 0:n, :, :].rearrange("p j u (b i) -> p j b u i", i=4),
                in_=xring[:, s:s + n, :].bitcast(F32).rearrange("p j (b i u) -> p j b u i", i=4, u=2),
            )

        def transposes(r):
            for j in range(ROUNDS[r]):
                s = (starts[r] + j) % X_SLOTS
                tp = psum.tile([P, 4, P], F32, name="tp", tag="tp%d" % j)
                tps[(r, j)] = tp
                for g in range(2):
                    for u in range(2):
                        if r < FIRST_PERMUTED:
                            words = xring[:, s, :].bitcast(F32)[:, 256 * g + u:256 * (g + 1):2]
                        else:
                            words = perms[r][:, j, u, g * P:(g + 1) * P]
                        nc.tensor.transpose(out=tp[:, 2 * g + u, :], in_=words, identity=ident[:])

        def copies(r):
            n = ROUNDS[r]
            if r not in grps:
                grps[r] = gpool.tile([P, MAXR * K], BF16, name="grp", tag="grp", align_bytes=ALIGN)
            gw = grps[r][:].bitcast(F32).rearrange("p (j g k u) -> p j g k u", j=MAXR, g=2, u=2)
            for j in range(n):
                src = tps[(r, j)][:].rearrange("p (g u) k -> p g k u", g=2)
                if r > 0 and j < (1 if n == 4 else (n + 1) // 2):
                    nc.vector.tensor_copy(out=gw[:, j, :, :, :], in_=src)
                else:
                    nc.scalar.copy(out=gw[:, j, :, :, :], in_=src)

        def quantise(r):
            n = ROUNDS[r]
            codes = cpool.tile([P, MAXR * 256], U32, name="codes", tag="codes", align_bytes=ALIGN)
            scl = cpool.tile([P, MAXR * 256], U8, name="scl", tag="scl", align_bytes=ALIGN)
            cods[r] = (codes, scl)
            nc.vector.quantize_mx(
                out=codes[:, 0:n * 256].bitcast(FP8X4),
                scales=scl[:, 0:n * 256],
                in_=grps[r][:, 0:n * K],
            )

        def multiply(r):
            n = ROUNDS[r]
            codes, scl = cods[r]
            for j in range(n):
                acc = psum.tile([P, N_OUT], F32, name="acc", tag="op%d" % j)
                for g in range(2):
                    o = (2 * j + g) * P
                    nc.tensor.matmul_mx(
                        out=acc[:],
                        lhsT=codes[:, o:o + P].bitcast(FP8X4),
                        lhsT_scale=scl[:, o:o + P],
                        rhs=wcodes[:, g, :].bitcast(FP8X4),
                        rhs_scale=wscl[:, g, :],
                        start=(g == 0),
                        stop=(g == 1),
                    )
                tps[("o", r, j)] = acc

        store_from = {}
        lo = 0
        for n in STORES:
            store_from[lo + n - 1] = lo
            lo += n

        def drain(r):
            for j in range(ROUNDS[r]):
                t = starts[r] + j
                s = t % O_SLOTS
                acc = tps[("o", r, j)]
                if j == 2:
                    nc.vector.tensor_copy(out=oring[:, s, :], in_=acc[:])
                else:
                    nc.scalar.copy(out=oring[:, s, :], in_=acc[:])
                if t in store_from:
                    lo = store_from[t]
                    nc.sync.dma_start(out=oview[:, lo:t + 1, :], in_=oring[:, s - (t - lo):s + 1, :])
                    if pending and pending[0][0] - O_SLOTS <= t + 1:
                        load()

        warm(WARM_FIRST)
        transposes(0)
        copies(0)
        weight_half(0)
        quantise(0)
        warm(WARM_BETWEEN)
        weight_half(1)
        for g in range(2):
            nc.vector.quantize_mx(out=wcodes[:, g, :].bitcast(FP8X4), scales=wscl[:, g, :], in_=wgrp[:, g, :])
        for r in range(n_rounds):
            if r + 1 < n_rounds:
                transposes(r + 1)
                copies(r + 1)
            if r == 0:
                warm(WARM_LAST)
            if r + 2 < n_rounds:
                permute(r + 2)
            multiply(r)
            if r + 1 < n_rounds:
                quantise(r + 1)
            drain(r)
